import numpy as np
import ml_dtypes


def mxq(x, axis, fmt="e4m3"):
    dtype, down = {"e4m3": (ml_dtypes.float8_e4m3fn, 7), "e5m2": (ml_dtypes.float8_e5m2, 14)}[fmt]
    v = np.moveaxis(np.asarray(x, np.float32).astype(ml_dtypes.bfloat16).astype(np.float64), axis, -1)
    blocks = v.reshape(v.shape[:-1] + (-1, 32))
    amax = np.abs(blocks).max(-1, keepdims=True)
    byte = np.maximum(np.where(amax > 0, np.frexp(amax)[1] - 1 + 127, 0) - down, 1)
    scale = np.exp2(byte - 127.0)
    codes = (blocks / scale).astype(np.float32).astype(dtype).astype(np.float64)
    return np.moveaxis((codes * scale).reshape(v.shape), -1, axis)


WIDE = False


def mx_kscale(k):
    if not WIDE:
        return np.ones(k)
    levels = np.array([10, -10, 5, -5, 0])
    a = np.random.permutation(np.resize(levels, k // 512 * 4)).reshape(k // 512, 4)
    idx = np.arange(k)
    return np.exp2(a[idx // 512, idx % 128 // 32])


BF16 = ml_dtypes.bfloat16


def bf(x):
    return np.asarray(x, np.float32).astype(BF16)


def f64(x):
    return np.asarray(x).astype(np.float64)


E2M1 = np.array([0.0, 0.5, 1.0, 1.5, 2.0, 3.0, 4.0, 6.0, -0.0, -0.5, -1.0, -1.5, -2.0, -3.0, -4.0, -6.0])


def pack_weight(w, fmt):
    k, n = w.shape
    w = f64(bf(w)).reshape(k // 32, 32, n)
    amax = np.abs(w).max(1)
    if fmt == "e4m3":
        byte = np.frexp(amax)[1] - 1 + 127 - 7
    else:
        mant, ex = np.frexp(amax / 6.0)
        byte = np.where(mant > 0.5, ex, ex - 1) + 127
    byte = np.clip(np.where(amax > 0, byte, 1), 1, 254)
    scaled = (w * np.exp2(127.0 - byte)[:, None, :]).reshape(k, n).astype(np.float32)
    by_word = np.ascontiguousarray(scaled.reshape(k // 512, 128, 4, n).transpose(0, 1, 3, 2))
    if fmt == "e4m3":
        words = by_word.astype(ml_dtypes.float8_e4m3fn).view(np.uint8)
    else:
        c = by_word.astype(ml_dtypes.float4_e2m1fn).view(np.uint8) & 0xF
        words = c[..., 0::2] | (c[..., 1::2] << 4)
    return np.ascontiguousarray(words), np.ascontiguousarray(byte.astype(np.uint8).reshape(k // 512, 16, n))


def unpack_weight(words, scales, fmt):
    g, p, n, _ = words.shape
    if fmt == "e4m3":
        vals = np.ascontiguousarray(words).view(ml_dtypes.float8_e4m3fn).astype(np.float64)
    else:
        nib = np.empty((g, p, n, 4), np.uint8)
        nib[..., 0::2] = words & 0xF
        nib[..., 1::2] = words >> 4
        vals = E2M1[nib]
    vals = vals * np.repeat(np.exp2(scales.astype(np.float64) - 127.0), 8, axis=1)[..., None]
    return vals.transpose(0, 1, 3, 2).reshape(g * 512, n)


B, S, E, H, KD, HD, C = 1, 256, 8192, 8, 128, 256, 512
W = H * KD
FMT = "e4m3"


def angles():
    lin = np.linspace(0.0, 1.0, KD // 2)
    angle = np.repeat(1.0 / (10000.0 ** lin), 2)
    idx = np.arange(S, dtype=np.float64)
    return np.sin(idx[:, None] * angle[None, :]), np.cos(idx[:, None] * angle[None, :])


def rotate_every_two(t):
    t1 = t[..., ::2]
    t2 = t[..., 1::2]
    return np.stack((-t2, t1), axis=-1).reshape(t.shape)


def setup_inputs():
    s = mx_kscale(E)
    x = bf(np.random.standard_normal((B, S, E)) * s)
    wq_words, wq_scales = pack_weight(np.random.standard_normal((E, W)) * 1.4 / np.sqrt(E) / s[:, None], FMT)
    wk_words, wk_scales = pack_weight(np.random.standard_normal((E, W)) * 1.4 / np.sqrt(E) / s[:, None], FMT)
    return {"x": x,
            "wq_words": wq_words, "wq_scales": wq_scales,
            "wk_words": wk_words, "wk_scales": wk_scales}


def reference(x, wq_words, wq_scales, wk_words, wk_scales):
    sin, cos = angles()
    xq = mxq(f64(x), 2, "e4m3")
    q = xq @ unpack_weight(wq_words, wq_scales, FMT)
    k = (xq @ unpack_weight(wk_words, wk_scales, FMT)) * KD ** -0.5
    q = q.reshape(B, S, H, KD).transpose(0, 2, 1, 3)
    k = k.reshape(B, S, H, KD).transpose(0, 2, 1, 3)
    q_rot = q * cos + rotate_every_two(q) * sin
    k_rot = k * cos + rotate_every_two(k) * sin
    return q_rot, k_rot

@@ -1,0 +1,308 @@
+import math
+from contextlib import ExitStack
+
+import concourse.mybir as mybir
+from concourse.masks import make_identity
+
+F32 = mybir.dt.float32
+BF16 = mybir.dt.bfloat16
+I32 = mybir.dt.int32
+U32 = mybir.dt.uint32
+U8 = mybir.dt.uint8
+FP8X4 = mybir.dt.float8_e4m3fn_x4
+ALU = mybir.AluOpType
+ACT = mybir.ActivationFunctionType
+
+P = 128
+TOKENS = 256
+TOKEN_TILES = TOKENS // P
+EMBED = 8192
+HEADS = 8
+HEAD_DIM = 128
+PAIRS = HEAD_DIM // 2
+DOUBLINGS = 6
+WIDTH = HEADS * HEAD_DIM
+PACK = 4
+K_PASS = P * PACK
+PASSES = EMBED // K_PASS
+N_TILE = 512
+HEADS_PER_BANK = N_TILE // HEAD_DIM
+X_PASSES = 4
+W_PASSES = 2
+PLANES = 4
+QUADRANT = 32
+FIRST_TRANSPOSE_BANK = 4
+
+FLOPS = 2 * TOKENS * EMBED * 2 * WIDTH
+
+assert 2**DOUBLINGS == PAIRS
+
+
+def build_rotation_tables(nc, keep, scale_of):
+    position_int = keep.tile([P, TOKEN_TILES], I32)
+    nc.gpsimd.iota(position_int, pattern=[[1, TOKEN_TILES]], base=0, channel_multiplier=TOKEN_TILES)
+    position = keep.tile([P, TOKEN_TILES], F32)
+    nc.vector.tensor_copy(out=position, in_=position_int)
+
+    ratio = 10000.0 ** (-1.0 / (PAIRS - 1))
+    angle = keep.tile([P, PAIRS], F32)
+    nc.vector.memset(angle[:, 0:1], 1.0)
+    for doubling in range(DOUBLINGS):
+        done = 2**doubling
+        nc.vector.tensor_scalar_mul(
+            out=angle[:, done : 2 * done], in0=angle[:, 0:done], scalar1=ratio**done
+        )
+
+    phase = keep.tile([P, TOKEN_TILES, 2, PAIRS], F32)
+    for m in range(TOKEN_TILES):
+        for kind, shift in enumerate((0.0, math.pi / 2)):
+            nc.vector.tensor_scalar(
+                out=phase[:, m, kind, :],
+                in0=angle,
+                scalar1=position[:, m : m + 1],
+                scalar2=shift,
+                op0=ALU.mult,
+                op1=ALU.add,
+            )
+
+    half_turns_int = keep.tile([P, TOKEN_TILES, 2, PAIRS], I32)
+    nc.vector.tensor_scalar_mul(out=half_turns_int, in0=phase, scalar1=1.0 / math.pi)
+    half_turns = keep.tile([P, TOKEN_TILES, 2, PAIRS], F32)
+    nc.vector.tensor_copy(out=half_turns, in_=half_turns_int)
+    pi_high = 3.140625
+    pi_low = math.pi - pi_high
+    reduced = keep.tile([P, TOKEN_TILES, 2, PAIRS], F32)
+    nc.vector.scalar_tensor_tensor(
+        out=reduced, in0=half_turns, scalar=-pi_high, in1=phase, op0=ALU.mult, op1=ALU.add
+    )
+    nc.vector.scalar_tensor_tensor(
+        out=reduced, in0=half_turns, scalar=-pi_low, in1=reduced, op0=ALU.mult, op1=ALU.add
+    )
+    sine = keep.tile([P, TOKEN_TILES, 2, PAIRS], F32)
+    nc.scalar.activation(out=sine, in_=reduced, func=ACT.Sin)
+
+    odd_int = keep.tile([P, TOKEN_TILES, 2, PAIRS], I32)
+    nc.vector.tensor_single_scalar(out=odd_int, in_=half_turns_int, scalar=1, op=ALU.bitwise_and)
+    sign = keep.tile([P, TOKEN_TILES, 2, PAIRS], F32)
+    nc.vector.tensor_scalar(
+        out=sign, in0=odd_int, scalar1=-2.0, scalar2=1.0, op0=ALU.mult, op1=ALU.add
+    )
+    trig = keep.tile([P, TOKEN_TILES, 2, PAIRS], F32)
+    nc.vector.tensor_tensor(out=trig, in0=sine, in1=sign, op=ALU.mult)
+
+    tables = {}
+    for name, scale in scale_of.items():
+        cos_pairs = keep.tile([P, TOKEN_TILES, PAIRS, 2], F32, name="cos_pairs_" + name)
+        nc.vector.tensor_scalar_mul(
+            out=cos_pairs,
+            in0=trig[:, :, 1, :].unsqueeze(3).to_broadcast([P, TOKEN_TILES, PAIRS, 2]),
+            scalar1=scale,
+        )
+        sin_cross = keep.tile([P, TOKEN_TILES, 2, PAIRS], F32, name="sin_cross_" + name)
+        nc.vector.tensor_scalar_mul(out=sin_cross[:, :, 0, :], in0=trig[:, :, 0, :], scalar1=-scale)
+        nc.vector.tensor_scalar_mul(out=sin_cross[:, :, 1, :], in0=trig[:, :, 0, :], scalar1=scale)
+        tables[name] = (cos_pairs, sin_cross)
+    return tables
+
+
+def load_scale_planes(nc, planes, scales, group):
+    for quadrant in range(P // QUADRANT):
+        first = QUADRANT * quadrant
+        nc.sync.dma_start(
+            out=planes[first : first + PACK * PLANES, group, :].bitcast(I32),
+            in_=scales[
+                PLANES * group : PLANES * (group + 1), PACK * quadrant : PACK * (quadrant + 1), :
+            ].bitcast(I32),
+        )
+
+
+def quantise_x_chunk(nc, grouped_pool, psum, identity, x_chunk, x_codes, x_scales):
+    words = x_chunk.bitcast(F32)
+    words_per_pass = K_PASS // 2
+    grouped = grouped_pool.tile([P, X_PASSES, TOKENS, PACK], BF16, align_bytes=64)
+    grouped_words = grouped.bitcast(F32)
+    for j in range(X_PASSES):
+        turned = psum.tile(
+            [P, TOKEN_TILES, 2, P], F32, tag="bank%d" % (FIRST_TRANSPOSE_BANK + j), name="turned"
+        )
+        for m in range(TOKEN_TILES):
+            for u in range(2):
+                nc.tensor.transpose(
+                    turned[:, m, u, :],
+                    words[:, m, words_per_pass * j + u : words_per_pass * (j + 1) : 2],
+                    identity,
+                )
+        copy_out = nc.vector.tensor_copy if j % 2 == 0 else nc.scalar.copy
+        copy_out(
+            out=grouped_words[:, j].rearrange("p (m r) u -> p m r u", m=TOKEN_TILES),
+            in_=turned.rearrange("p m u r -> p m r u"),
+        )
+    nc.vector.quantize_mx(
+        out=x_codes.rearrange("p g r -> p (g r)").bitcast(FP8X4),
+        scales=x_scales.rearrange("p g r -> p (g r)"),
+        in_=grouped.rearrange("p g r t -> p (g r t)"),
+    )
+
+
+def multiply_chunk(nc, w_pool, words, planes, first_column, first_pass, x_codes, x_scales, sums):
+    width = N_TILE * len(sums)
+    w = w_pool.tile([P, W_PASSES, width], U32, tag="w", align_bytes=64)
+    nc.sync.dma_start(
+        out=w.bitcast(I32),
+        in_=words[:, first_pass : first_pass + W_PASSES, first_column : first_column + width],
+    )
+    for n in range(len(sums)):
+        for m in range(TOKEN_TILES):
+            for i in range(W_PASSES):
+                g = first_pass + i
+                plane_start = PACK * (g % PLANES)
+                nc.tensor.matmul_mx(
+                    out=sums[n][m],
+                    lhsT=x_codes[:, g, P * m : P * (m + 1)].bitcast(FP8X4),
+                    lhsT_scale=x_scales[:, g, P * m : P * (m + 1)],
+                    rhs=w[:, i, N_TILE * n : N_TILE * (n + 1)].bitcast(FP8X4),
+                    rhs_scale=planes[
+                        plane_start:P,
+                        g // PLANES,
+                        first_column + N_TILE * n : first_column + N_TILE * (n + 1),
+                    ],
+                    start=(g == 0),
+                    stop=(g == PASSES - 1),
+                )
+
+
+def rotate_bank(nc, cross_pool, bank, cos_pairs, sin_cross, rotated):
+    by_head = bank.rearrange("p (h f) -> p h f", h=HEADS_PER_BANK)
+    by_pair = bank.rearrange("p (h c e) -> p h c e", h=HEADS_PER_BANK, e=2)
+    nc.vector.tensor_tensor(
+        out=rotated,
+        in0=by_head,
+        in1=cos_pairs.rearrange("p c e -> p (c e)")
+        .unsqueeze(1)
+        .to_broadcast([P, HEADS_PER_BANK, HEAD_DIM]),
+        op=ALU.mult,
+    )
+    cross = cross_pool.tile([P, 2, HEADS_PER_BANK, PAIRS], F32)
+    for e in range(2):
+        nc.vector.tensor_tensor(
+            out=cross[:, e],
+            in0=by_pair[:, :, :, 1 - e],
+            in1=sin_cross[:, e, :].unsqueeze(1).to_broadcast([P, HEADS_PER_BANK, PAIRS]),
+            op=ALU.mult,
+        )
+    rotated_pairs = rotated.rearrange("p h (c e) -> p h c e", e=2)
+    nc.vector.tensor_tensor(
+        out=rotated_pairs,
+        in0=rotated_pairs,
+        in1=cross.rearrange("p e h c -> p h c e"),
+        op=ALU.add,
+    )
+
+
+def tile_retnet_pa_k_kernel(tc, x, wq_words, wq_scales, wk_words, wk_scales, out_0, out_1):
+    nc = tc.nc
+    with ExitStack() as ctx:
+        ctx.enter_context(tc.manual_schedule())
+        keep = ctx.enter_context(tc.tile_pool(name="keep", bufs=1))
+        x_pool = ctx.enter_context(tc.tile_pool(name="x", bufs=2))
+        grouped_pool = ctx.enter_context(tc.tile_pool(name="grouped", bufs=2))
+        w_pool = ctx.enter_context(tc.tile_pool(name="w", bufs=12))
+        cross_pool = ctx.enter_context(tc.tile_pool(name="cross", bufs=2))
+        psum = ctx.enter_context(tc.psum_pool(name="psum", bufs=1))
+
+        x_rows = x.rearrange("b (p m) k -> p (b m) k", m=TOKEN_TILES)
+        words_of = {
+            "q": wq_words.rearrange("g p n t -> p g (n t)").bitcast(I32),
+            "k": wk_words.rearrange("g p n t -> p g (n t)").bitcast(I32),
+        }
+        scales_of = {"q": wq_scales, "k": wk_scales}
+        out_of = {
+            "q": out_0.rearrange("b h (p m) f -> p (b h) (m f)", m=TOKEN_TILES),
+            "k": out_1.rearrange("b h (p m) f -> p (b h) (m f)", m=TOKEN_TILES),
+        }
+
+        planes_of = {}
+        for name in ("q", "k"):
+            planes_of[name] = keep.tile(
+                [P, PASSES // PLANES, WIDTH], U8, name="planes_" + name, align_bytes=64
+            )
+            nc.vector.memset(planes_of[name].bitcast(I32), 0)
+
+        identity = keep.tile([P, P], F32)
+        make_identity(nc, identity)
+        tables = build_rotation_tables(nc, keep, {"q": 1.0, "k": HEAD_DIM**-0.5})
+
+        x_codes = keep.tile([P, PASSES, TOKENS], U32, align_bytes=64)
+        x_scales = keep.tile([P, PASSES, TOKENS], U8, align_bytes=64)
+
+        def open_sums(first_bank, n_tiles):
+            return [
+                [
+                    psum.tile(
+                        [P, N_TILE], F32, tag="bank%d" % (first_bank + TOKEN_TILES * n + m), name="sums"
+                    )
+                    for m in range(TOKEN_TILES)
+                ]
+                for n in range(n_tiles)
+            ]
+
+        stores = []
+
+        def rotate_block(name, first_column, sums):
+            cos_pairs, sin_cross = tables[name]
+            for n in range(len(sums)):
+                rotated = keep.tile(
+                    [P, HEADS_PER_BANK, TOKEN_TILES, HEAD_DIM],
+                    F32,
+                    name="rotated_%s_%d" % (name, first_column + N_TILE * n),
+                )
+                for m in range(TOKEN_TILES):
+                    rotate_bank(
+                        nc, cross_pool, sums[n][m], cos_pairs[:, m], sin_cross[:, m], rotated[:, :, m, :]
+                    )
+                first_head = (first_column + N_TILE * n) // HEAD_DIM
+                stores.append((out_of[name][:, first_head : first_head + HEADS_PER_BANK, :], rotated))
+
+        def load_and_quantise_x(group):
+            first_pass = X_PASSES * group
+            x_chunk = x_pool.tile([P, TOKEN_TILES, X_PASSES * K_PASS], BF16)
+            nc.sync.dma_start(
+                out=x_chunk, in_=x_rows[:, :, K_PASS * first_pass : K_PASS * (first_pass + X_PASSES)]
+            )
+            quantise_x_chunk(
+                nc,
+                grouped_pool,
+                psum,
+                identity,
+                x_chunk,
+                x_codes[:, first_pass : first_pass + X_PASSES, :],
+                x_scales[:, first_pass : first_pass + X_PASSES, :],
+            )
+
+        sums = open_sums(0, WIDTH // N_TILE)
+        x_groups = PASSES // X_PASSES
+        load_and_quantise_x(0)
+        for group in range(x_groups):
+            first_pass = X_PASSES * group
+            load_scale_planes(nc, planes_of["q"], scales_of["q"], group)
+            if group + 1 < x_groups:
+                load_and_quantise_x(group + 1)
+            for chunk_pass in range(first_pass, first_pass + X_PASSES, W_PASSES):
+                multiply_chunk(
+                    nc, w_pool, words_of["q"], planes_of["q"], 0, chunk_pass, x_codes, x_scales, sums
+                )
+        rotate_block("q", 0, sums)
+
+        for group in range(PASSES // PLANES):
+            load_scale_planes(nc, planes_of["k"], scales_of["k"], group)
+        for half in range(WIDTH // N_TILE):
+            first_column = N_TILE * half
+            sums = open_sums(FIRST_TRANSPOSE_BANK + TOKEN_TILES * half, 1)
+            for chunk_pass in range(0, PASSES, W_PASSES):
+                multiply_chunk(
+                    nc, w_pool, words_of["k"], planes_of["k"], first_column, chunk_pass, x_codes, x_scales, sums
+                )
+            rotate_block("k", first_column, sums)
+
+        for destination, rotated in stores:
+            nc.sync.dma_start(out=destination, in_=rotated.rearrange("p h m f -> p h (m f)"))

@@ -108,11 +108,11 @@ def build_rotation_tables(nc, keep, scale_of):
 def load_scale_planes(nc, planes, scales, group):
     for quadrant in range(P // QUADRANT):
         first = QUADRANT * quadrant
-        nc.sync.dma_start(
-            out=planes[first : first + PACK * PLANES, group, :].bitcast(I32),
+        nc.gpsimd.dma_start(
+            out=planes[first : first + PACK * PLANES, group, :].bitcast(F32),
             in_=scales[
                 PLANES * group : PLANES * (group + 1), PACK * quadrant : PACK * (quadrant + 1), :
-            ].bitcast(I32),
+            ].bitcast(F32),
         )
 
 
@@ -231,6 +231,9 @@ def tile_retnet_pa_k_kernel(tc, x, wq_words, wq_scales, wk_words, wk_scales, out
         identity = keep.tile([P, P], F32)
         make_identity(nc, identity)
         tables = build_rotation_tables(nc, keep, {"q": 1.0, "k": HEAD_DIM**-0.5})
+        for name in ("q", "k"):
+            for group in range(PASSES // PLANES):
+                load_scale_planes(nc, planes_of[name], scales_of[name], group)
 
         x_codes = keep.tile([P, PASSES, TOKENS], U32, align_bytes=64)
         x_scales = keep.tile([P, PASSES, TOKENS], U8, align_bytes=64)
@@ -284,7 +287,6 @@ def tile_retnet_pa_k_kernel(tc, x, wq_words, wq_scales, wk_words, wk_scales, out
         load_and_quantise_x(0)
         for group in range(x_groups):
             first_pass = X_PASSES * group
-            load_scale_planes(nc, planes_of["q"], scales_of["q"], group)
             if group + 1 < x_groups:
                 load_and_quantise_x(group + 1)
             for chunk_pass in range(first_pass, first_pass + X_PASSES, W_PASSES):
@@ -293,8 +295,6 @@ def tile_retnet_pa_k_kernel(tc, x, wq_words, wq_scales, wk_words, wk_scales, out
                 )
         rotate_block("q", 0, sums)
 
-        for group in range(PASSES // PLANES):
-            load_scale_planes(nc, planes_of["k"], scales_of["k"], group)
         for half in range(WIDTH // N_TILE):
             first_column = N_TILE * half
             sums = open_sums(FIRST_TRANSPOSE_BANK + TOKEN_TILES * half, 1)

@@ -116,9 +116,12 @@ def load_scale_planes(nc, planes, scales, group):
         )
 
 
-def quantise_x_chunk(nc, grouped_pool, psum, identity, x_chunk, x_codes, x_scales):
+def quantise_x_chunk(nc, sorted_pool, grouped_pool, psum, identity, x_chunk, x_codes, x_scales):
     words = x_chunk.bitcast(F32)
-    words_per_pass = K_PASS // 2
+    sorted_words = sorted_pool.tile([P, TOKEN_TILES, X_PASSES, 2, P], F32)
+    for m in range(TOKEN_TILES):
+        sort = nc.vector.tensor_copy if m % 2 == 0 else nc.scalar.copy
+        sort(out=sorted_words[:, m], in_=words[:, m].rearrange("p (j w u) -> p j u w", w=P, u=2))
     grouped = grouped_pool.tile([P, X_PASSES, TOKENS, PACK], BF16, align_bytes=64)
     grouped_words = grouped.bitcast(F32)
     for j in range(X_PASSES):
@@ -127,11 +130,7 @@ def quantise_x_chunk(nc, grouped_pool, psum, identity, x_chunk, x_codes, x_scale
         )
         for m in range(TOKEN_TILES):
             for u in range(2):
-                nc.tensor.transpose(
-                    turned[:, m, u, :],
-                    words[:, m, words_per_pass * j + u : words_per_pass * (j + 1) : 2],
-                    identity,
-                )
+                nc.tensor.transpose(turned[:, m, u, :], sorted_words[:, m, j, u, :], identity)
         copy_out = nc.vector.tensor_copy if j % 2 == 0 else nc.scalar.copy
         copy_out(
             out=grouped_words[:, j].rearrange("p (m r) u -> p m r u", m=TOKEN_TILES),
@@ -205,6 +204,7 @@ def tile_retnet_pa_k_kernel(tc, x, wq_words, wq_scales, wk_words, wk_scales, out
         ctx.enter_context(tc.manual_schedule())
         keep = ctx.enter_context(tc.tile_pool(name="keep", bufs=1))
         x_pool = ctx.enter_context(tc.tile_pool(name="x", bufs=2))
+        sorted_pool = ctx.enter_context(tc.tile_pool(name="sorted", bufs=2))
         grouped_pool = ctx.enter_context(tc.tile_pool(name="grouped", bufs=2))
         w_pool = ctx.enter_context(tc.tile_pool(name="w", bufs=12))
         cross_pool = ctx.enter_context(tc.tile_pool(name="cross", bufs=2))
@@ -274,6 +274,7 @@ def tile_retnet_pa_k_kernel(tc, x, wq_words, wq_scales, wk_words, wk_scales, out
             )
             quantise_x_chunk(
                 nc,
+                sorted_pool,
                 grouped_pool,
                 psum,
                 identity,

@@ -38,9 +38,7 @@ FLOPS = 2 * TOKENS * EMBED * 2 * WIDTH
 assert 2**DOUBLINGS == PAIRS
 
 
-def build_rotation_tables(nc, keep, scale_of):
-    position_int = keep.tile([P, TOKEN_TILES], I32)
-    nc.gpsimd.iota(position_int, pattern=[[1, TOKEN_TILES]], base=0, channel_multiplier=TOKEN_TILES)
+def build_rotation_tables(nc, keep, position_int, scale_of):
     position = keep.tile([P, TOKEN_TILES], F32)
     nc.vector.tensor_copy(out=position, in_=position_int)
 
@@ -230,7 +228,10 @@ def tile_retnet_pa_k_kernel(tc, x, wq_words, wq_scales, wk_words, wk_scales, out
 
         identity = keep.tile([P, P], F32)
         make_identity(nc, identity)
-        tables = build_rotation_tables(nc, keep, {"q": 1.0, "k": HEAD_DIM**-0.5})
+        position_int = keep.tile([P, TOKEN_TILES], I32)
+        nc.gpsimd.iota(
+            position_int, pattern=[[1, TOKEN_TILES]], base=0, channel_multiplier=TOKEN_TILES
+        )
         for name in ("q", "k"):
             for group in range(PASSES // PLANES):
                 load_scale_planes(nc, planes_of[name], scales_of[name], group)
@@ -249,9 +250,13 @@ def tile_retnet_pa_k_kernel(tc, x, wq_words, wq_scales, wk_words, wk_scales, out
                 for n in range(n_tiles)
             ]
 
+        zero = keep.tile([P, 1], F32)
+        nc.vector.memset(zero, 0.0)
+        nc.scalar.activation(out=zero, in_=zero, func=ACT.Sin)
+
         stores = []
 
-        def rotate_block(name, first_column, sums):
+        def rotate_block(name, first_column, sums, tables):
             cos_pairs, sin_cross = tables[name]
             for n in range(len(sums)):
                 rotated = keep.tile(
@@ -294,7 +299,8 @@ def tile_retnet_pa_k_kernel(tc, x, wq_words, wq_scales, wk_words, wk_scales, out
                 multiply_chunk(
                     nc, w_pool, words_of["q"], planes_of["q"], 0, chunk_pass, x_codes, x_scales, sums
                 )
-        rotate_block("q", 0, sums)
+        tables = build_rotation_tables(nc, keep, position_int, {"q": 1.0, "k": HEAD_DIM**-0.5})
+        rotate_block("q", 0, sums, tables)
 
         for half in range(WIDTH // N_TILE):
             first_column = N_TILE * half
@@ -303,7 +309,7 @@ def tile_retnet_pa_k_kernel(tc, x, wq_words, wq_scales, wk_words, wk_scales, out
                 multiply_chunk(
                     nc, w_pool, words_of["k"], planes_of["k"], first_column, chunk_pass, x_codes, x_scales, sums
                 )
-            rotate_block("k", first_column, sums)
+            rotate_block("k", first_column, sums, tables)
 
         for destination, rotated in stores:
             nc.sync.dma_start(out=destination, in_=rotated.rearrange("p h m f -> p h (m f)"))

@@ -27,7 +27,8 @@ K_PASS = P * PACK
 PASSES = EMBED // K_PASS
 N_TILE = 512
 HEADS_PER_BANK = N_TILE // HEAD_DIM
-X_PASSES = 4
+X_CHUNKS = (1, 1, 2, 4, 4, 4)
+MAX_X_PASSES = 4
 W_PASSES = 2
 PLANES = 4
 QUADRANT = 32
@@ -36,6 +37,7 @@ FIRST_TRANSPOSE_BANK = 4
 FLOPS = 2 * TOKENS * EMBED * 2 * WIDTH
 
 assert 2**DOUBLINGS == PAIRS
+assert sum(X_CHUNKS) == PASSES and max(X_CHUNKS) <= MAX_X_PASSES
 
 
 def build_rotation_tables(nc, keep, position_int, scale_of):
@@ -103,10 +105,10 @@ def build_rotation_tables(nc, keep, position_int, scale_of):
     return tables
 
 
-def load_scale_planes(nc, planes, scales, group):
+def load_scale_planes(queue, planes, scales, group):
     for quadrant in range(P // QUADRANT):
         first = QUADRANT * quadrant
-        nc.gpsimd.dma_start(
+        queue.dma_start(
             out=planes[first : first + PACK * PLANES, group, :].bitcast(F32),
             in_=scales[
                 PLANES * group : PLANES * (group + 1), PACK * quadrant : PACK * (quadrant + 1), :
@@ -114,26 +116,34 @@ def load_scale_planes(nc, planes, scales, group):
         )
 
 
-def quantise_x_chunk(nc, sorted_pool, grouped_pool, psum, identity, x_chunk, x_codes, x_scales):
+def turn_x_chunk(nc, sorted_pool, grouped_pool, psum, identity, x_chunk, first_pass, passes):
     words = x_chunk.bitcast(F32)
-    sorted_words = sorted_pool.tile([P, TOKEN_TILES, X_PASSES, 2, P], F32)
-    for m in range(TOKEN_TILES):
-        sort = nc.vector.tensor_copy if m % 2 == 0 else nc.scalar.copy
-        sort(out=sorted_words[:, m], in_=words[:, m].rearrange("p (j w u) -> p j u w", w=P, u=2))
-    grouped = grouped_pool.tile([P, X_PASSES, TOKENS, PACK], BF16, align_bytes=64)
+    if passes > 1:
+        sorted_words = sorted_pool.tile([P, TOKEN_TILES, passes, 2, P], F32, tag="sorted_words")
+        for m in range(TOKEN_TILES):
+            sort = nc.vector.tensor_copy if m % 2 == 0 else nc.scalar.copy
+            sort(out=sorted_words[:, m], in_=words[:, m].rearrange("p (j w u) -> p j u w", w=P, u=2))
+    grouped = grouped_pool.tile([P, passes, TOKENS, PACK], BF16, tag="grouped", align_bytes=64)
     grouped_words = grouped.bitcast(F32)
-    for j in range(X_PASSES):
-        turned = psum.tile(
-            [P, TOKEN_TILES, 2, P], F32, tag="bank%d" % (FIRST_TRANSPOSE_BANK + j), name="turned"
-        )
+    for j in range(passes):
+        bank = FIRST_TRANSPOSE_BANK + (first_pass + j) % MAX_X_PASSES
+        turned = psum.tile([P, TOKEN_TILES, 2, P], F32, tag="bank%d" % bank, name="turned")
         for m in range(TOKEN_TILES):
             for u in range(2):
-                nc.tensor.transpose(turned[:, m, u, :], sorted_words[:, m, j, u, :], identity)
-        copy_out = nc.vector.tensor_copy if j % 2 == 0 else nc.scalar.copy
+                if passes > 1:
+                    source = sorted_words[:, m, j, u, :]
+                else:
+                    source = words[:, m, u : 2 * P : 2]
+                nc.tensor.transpose(turned[:, m, u, :], source, identity)
+        copy_out = nc.vector.tensor_copy if (j % 2 == 0 and passes > 1) else nc.scalar.copy
         copy_out(
             out=grouped_words[:, j].rearrange("p (m r) u -> p m r u", m=TOKEN_TILES),
             in_=turned.rearrange("p m u r -> p m r u"),
         )
+    return grouped
+
+
+def quantise_x_chunk(nc, grouped, x_codes, x_scales):
     nc.vector.quantize_mx(
         out=x_codes.rearrange("p g r -> p (g r)").bitcast(FP8X4),
         scales=x_scales.rearrange("p g r -> p (g r)"),
@@ -141,16 +151,20 @@ def quantise_x_chunk(nc, sorted_pool, grouped_pool, psum, identity, x_chunk, x_c
     )
 
 
-def multiply_chunk(nc, w_pool, words, planes, first_column, first_pass, x_codes, x_scales, sums):
-    width = N_TILE * len(sums)
-    w = w_pool.tile([P, W_PASSES, width], U32, tag="w", align_bytes=64)
+def load_weights(nc, w_pool, words, first_column, n_tiles, first_pass, passes):
+    width = N_TILE * n_tiles
+    w = w_pool.tile([P, passes, width], U32, tag="w", align_bytes=64)
     nc.sync.dma_start(
         out=w.bitcast(I32),
-        in_=words[:, first_pass : first_pass + W_PASSES, first_column : first_column + width],
+        in_=words[:, first_pass : first_pass + passes, first_column : first_column + width],
     )
+    return w
+
+
+def multiply(nc, w, planes, first_column, first_pass, passes, x_codes, x_scales, sums):
     for n in range(len(sums)):
         for m in range(TOKEN_TILES):
-            for i in range(W_PASSES):
+            for i in range(passes):
                 g = first_pass + i
                 plane_start = PACK * (g % PLANES)
                 nc.tensor.matmul_mx(
@@ -201,7 +215,6 @@ def tile_retnet_pa_k_kernel(tc, x, wq_words, wq_scales, wk_words, wk_scales, out
     with ExitStack() as ctx:
         ctx.enter_context(tc.manual_schedule())
         keep = ctx.enter_context(tc.tile_pool(name="keep", bufs=1))
-        x_pool = ctx.enter_context(tc.tile_pool(name="x", bufs=2))
         sorted_pool = ctx.enter_context(tc.tile_pool(name="sorted", bufs=2))
         grouped_pool = ctx.enter_context(tc.tile_pool(name="grouped", bufs=2))
         w_pool = ctx.enter_context(tc.tile_pool(name="w", bufs=12))
@@ -224,7 +237,12 @@ def tile_retnet_pa_k_kernel(tc, x, wq_words, wq_scales, wk_words, wk_scales, out
             planes_of[name] = keep.tile(
                 [P, PASSES // PLANES, WIDTH], U8, name="planes_" + name, align_bytes=64
             )
-            nc.vector.memset(planes_of[name].bitcast(I32), 0)
+        zero = keep.tile([P, 1], F32)
+        nc.vector.memset(planes_of["q"][:, 0, :].bitcast(I32), 0)
+        nc.vector.memset(zero, 0.0)
+        nc.vector.memset(planes_of["q"][:, 1:, :].bitcast(I32), 0)
+        nc.vector.memset(planes_of["k"].bitcast(I32), 0)
+        load_scale_planes(nc.scalar, planes_of["q"], scales_of["q"], 0)
 
         identity = keep.tile([P, P], F32)
         make_identity(nc, identity)
@@ -234,7 +252,8 @@ def tile_retnet_pa_k_kernel(tc, x, wq_words, wq_scales, wk_words, wk_scales, out
         )
         for name in ("q", "k"):
             for group in range(PASSES // PLANES):
-                load_scale_planes(nc, planes_of[name], scales_of[name], group)
+                if (name, group) != ("q", 0):
+                    load_scale_planes(nc.gpsimd, planes_of[name], scales_of[name], group)
 
         x_codes = keep.tile([P, PASSES, TOKENS], U32, align_bytes=64)
         x_scales = keep.tile([P, PASSES, TOKENS], U8, align_bytes=64)
@@ -250,8 +269,6 @@ def tile_retnet_pa_k_kernel(tc, x, wq_words, wq_scales, wk_words, wk_scales, out
                 for n in range(n_tiles)
             ]
 
-        zero = keep.tile([P, 1], F32)
-        nc.vector.memset(zero, 0.0)
         nc.scalar.activation(out=zero, in_=zero, func=ACT.Sin)
 
         stores = []
@@ -271,44 +288,54 @@ def tile_retnet_pa_k_kernel(tc, x, wq_words, wq_scales, wk_words, wk_scales, out
                 first_head = (first_column + N_TILE * n) // HEAD_DIM
                 stores.append((out_of[name][:, first_head : first_head + HEADS_PER_BANK, :], rotated))
 
-        def load_and_quantise_x(group):
-            first_pass = X_PASSES * group
-            x_chunk = x_pool.tile([P, TOKEN_TILES, X_PASSES * K_PASS], BF16)
+        first_pass_of = [sum(X_CHUNKS[:c]) for c in range(len(X_CHUNKS))]
+        x_chunks = {}
+
+        def load_x(c):
+            first_k = K_PASS * first_pass_of[c]
+            x_chunks[c] = keep.tile([P, TOKEN_TILES, X_CHUNKS[c] * K_PASS], BF16, name="x_chunk_%d" % c)
             nc.sync.dma_start(
-                out=x_chunk, in_=x_rows[:, :, K_PASS * first_pass : K_PASS * (first_pass + X_PASSES)]
+                out=x_chunks[c], in_=x_rows[:, :, first_k : first_k + X_CHUNKS[c] * K_PASS]
+            )
+
+        def turn_and_quantise_x(c):
+            first_pass = first_pass_of[c]
+            grouped = turn_x_chunk(
+                nc, sorted_pool, grouped_pool, psum, identity, x_chunks[c], first_pass, X_CHUNKS[c]
             )
             quantise_x_chunk(
                 nc,
-                sorted_pool,
-                grouped_pool,
-                psum,
-                identity,
-                x_chunk,
-                x_codes[:, first_pass : first_pass + X_PASSES, :],
-                x_scales[:, first_pass : first_pass + X_PASSES, :],
+                grouped,
+                x_codes[:, first_pass : first_pass + X_CHUNKS[c], :],
+                x_scales[:, first_pass : first_pass + X_CHUNKS[c], :],
             )
 
         sums = open_sums(0, WIDTH // N_TILE)
-        x_groups = PASSES // X_PASSES
-        load_and_quantise_x(0)
-        for group in range(x_groups):
-            first_pass = X_PASSES * group
-            if group + 1 < x_groups:
-                load_and_quantise_x(group + 1)
-            for chunk_pass in range(first_pass, first_pass + X_PASSES, W_PASSES):
-                multiply_chunk(
-                    nc, w_pool, words_of["q"], planes_of["q"], 0, chunk_pass, x_codes, x_scales, sums
+        load_x(0)
+        load_x(1)
+        turn_and_quantise_x(0)
+        for c in range(len(X_CHUNKS)):
+            loaded = []
+            for first_pass in range(first_pass_of[c], first_pass_of[c] + X_CHUNKS[c], W_PASSES):
+                passes = min(W_PASSES, X_CHUNKS[c])
+                loaded.append(
+                    (first_pass, passes, load_weights(nc, w_pool, words_of["q"], 0, len(sums), first_pass, passes))
                 )
+            if c + 2 < len(X_CHUNKS):
+                load_x(c + 2)
+            if c + 1 < len(X_CHUNKS):
+                turn_and_quantise_x(c + 1)
+            for first_pass, passes, w in loaded:
+                multiply(nc, w, planes_of["q"], 0, first_pass, passes, x_codes, x_scales, sums)
         tables = build_rotation_tables(nc, keep, position_int, {"q": 1.0, "k": HEAD_DIM**-0.5})
         rotate_block("q", 0, sums, tables)
 
         for half in range(WIDTH // N_TILE):
             first_column = N_TILE * half
             sums = open_sums(FIRST_TRANSPOSE_BANK + TOKEN_TILES * half, 1)
-            for chunk_pass in range(0, PASSES, W_PASSES):
-                multiply_chunk(
-                    nc, w_pool, words_of["k"], planes_of["k"], first_column, chunk_pass, x_codes, x_scales, sums
-                )
+            for first_pass in range(0, PASSES, W_PASSES):
+                w = load_weights(nc, w_pool, words_of["k"], first_column, 1, first_pass, W_PASSES)
+                multiply(nc, w, planes_of["k"], first_column, first_pass, W_PASSES, x_codes, x_scales, sums)
             rotate_block("k", first_column, sums, tables)
 
         for destination, rotated in stores:

@@ -30,6 +30,7 @@ HEADS_PER_BANK = N_TILE // HEAD_DIM
 X_CHUNKS = (1, 1, 2, 4, 4, 4)
 MAX_X_PASSES = 4
 W_PASSES = 2
+K_BLOCKS = ((512, 2, 4), (256, 4, 6), (256, 2, 0))
 PLANES = 4
 QUADRANT = 32
 FIRST_TRANSPOSE_BANK = 4
@@ -151,8 +152,7 @@ def quantise_x_chunk(nc, grouped, x_codes, x_scales):
     )
 
 
-def load_weights(nc, w_pool, words, first_column, n_tiles, first_pass, passes):
-    width = N_TILE * n_tiles
+def load_weights(nc, w_pool, words, first_column, width, first_pass, passes):
     w = w_pool.tile([P, passes, width], U32, tag="w", align_bytes=64)
     nc.sync.dma_start(
         out=w.bitcast(I32),
@@ -161,7 +161,7 @@ def load_weights(nc, w_pool, words, first_column, n_tiles, first_pass, passes):
     return w
 
 
-def multiply(nc, w, planes, first_column, first_pass, passes, x_codes, x_scales, sums):
+def multiply(nc, w, planes, first_column, tile_width, first_pass, passes, x_codes, x_scales, sums):
     for n in range(len(sums)):
         for m in range(TOKEN_TILES):
             for i in range(passes):
@@ -171,34 +171,34 @@ def multiply(nc, w, planes, first_column, first_pass, passes, x_codes, x_scales,
                     out=sums[n][m],
                     lhsT=x_codes[:, g, P * m : P * (m + 1)].bitcast(FP8X4),
                     lhsT_scale=x_scales[:, g, P * m : P * (m + 1)],
-                    rhs=w[:, i, N_TILE * n : N_TILE * (n + 1)].bitcast(FP8X4),
+                    rhs=w[:, i, tile_width * n : tile_width * (n + 1)].bitcast(FP8X4),
                     rhs_scale=planes[
                         plane_start:P,
                         g // PLANES,
-                        first_column + N_TILE * n : first_column + N_TILE * (n + 1),
+                        first_column + tile_width * n : first_column + tile_width * (n + 1),
                     ],
                     start=(g == 0),
                     stop=(g == PASSES - 1),
                 )
 
 
-def rotate_bank(nc, cross_pool, bank, cos_pairs, sin_cross, rotated):
-    by_head = bank.rearrange("p (h f) -> p h f", h=HEADS_PER_BANK)
-    by_pair = bank.rearrange("p (h c e) -> p h c e", h=HEADS_PER_BANK, e=2)
+def rotate_bank(nc, cross_pool, bank, heads, cos_pairs, sin_cross, rotated):
+    by_head = bank.rearrange("p (h f) -> p h f", h=heads)
+    by_pair = bank.rearrange("p (h c e) -> p h c e", h=heads, e=2)
     nc.vector.tensor_tensor(
         out=rotated,
         in0=by_head,
         in1=cos_pairs.rearrange("p c e -> p (c e)")
         .unsqueeze(1)
-        .to_broadcast([P, HEADS_PER_BANK, HEAD_DIM]),
+        .to_broadcast([P, heads, HEAD_DIM]),
         op=ALU.mult,
     )
-    cross = cross_pool.tile([P, 2, HEADS_PER_BANK, PAIRS], F32)
+    cross = cross_pool.tile([P, 2, heads, PAIRS], F32)
     for e in range(2):
         nc.vector.tensor_tensor(
             out=cross[:, e],
             in0=by_pair[:, :, :, 1 - e],
-            in1=sin_cross[:, e, :].unsqueeze(1).to_broadcast([P, HEADS_PER_BANK, PAIRS]),
+            in1=sin_cross[:, e, :].unsqueeze(1).to_broadcast([P, heads, PAIRS]),
             op=ALU.mult,
         )
     rotated_pairs = rotated.rearrange("p h (c e) -> p h c e", e=2)
@@ -258,11 +258,11 @@ def tile_retnet_pa_k_kernel(tc, x, wq_words, wq_scales, wk_words, wk_scales, out
         x_codes = keep.tile([P, PASSES, TOKENS], U32, align_bytes=64)
         x_scales = keep.tile([P, PASSES, TOKENS], U8, align_bytes=64)
 
-        def open_sums(first_bank, n_tiles):
+        def open_sums(first_bank, n_tiles, tile_width):
             return [
                 [
                     psum.tile(
-                        [P, N_TILE], F32, tag="bank%d" % (first_bank + TOKEN_TILES * n + m), name="sums"
+                        [P, tile_width], F32, tag="bank%d" % (first_bank + TOKEN_TILES * n + m), name="sums"
                     )
                     for m in range(TOKEN_TILES)
                 ]
@@ -273,20 +273,21 @@ def tile_retnet_pa_k_kernel(tc, x, wq_words, wq_scales, wk_words, wk_scales, out
 
         stores = []
 
-        def rotate_block(name, first_column, sums, tables):
+        def rotate_block(name, first_column, tile_width, sums, tables):
             cos_pairs, sin_cross = tables[name]
+            heads = tile_width // HEAD_DIM
             for n in range(len(sums)):
                 rotated = keep.tile(
-                    [P, HEADS_PER_BANK, TOKEN_TILES, HEAD_DIM],
+                    [P, heads, TOKEN_TILES, HEAD_DIM],
                     F32,
-                    name="rotated_%s_%d" % (name, first_column + N_TILE * n),
+                    name="rotated_%s_%d" % (name, first_column + tile_width * n),
                 )
                 for m in range(TOKEN_TILES):
                     rotate_bank(
-                        nc, cross_pool, sums[n][m], cos_pairs[:, m], sin_cross[:, m], rotated[:, :, m, :]
+                        nc, cross_pool, sums[n][m], heads, cos_pairs[:, m], sin_cross[:, m], rotated[:, :, m, :]
                     )
-                first_head = (first_column + N_TILE * n) // HEAD_DIM
-                stores.append((out_of[name][:, first_head : first_head + HEADS_PER_BANK, :], rotated))
+                first_head = (first_column + tile_width * n) // HEAD_DIM
+                stores.append((out_of[name][:, first_head : first_head + heads, :], rotated))
 
         first_pass_of = [sum(X_CHUNKS[:c]) for c in range(len(X_CHUNKS))]
         x_chunks = {}
@@ -310,7 +311,7 @@ def tile_retnet_pa_k_kernel(tc, x, wq_words, wq_scales, wk_words, wk_scales, out
                 x_scales[:, first_pass : first_pass + X_CHUNKS[c], :],
             )
 
-        sums = open_sums(0, WIDTH // N_TILE)
+        sums = open_sums(0, WIDTH // N_TILE, N_TILE)
         load_x(0)
         load_x(1)
         turn_and_quantise_x(0)
@@ -319,24 +320,25 @@ def tile_retnet_pa_k_kernel(tc, x, wq_words, wq_scales, wk_words, wk_scales, out
             for first_pass in range(first_pass_of[c], first_pass_of[c] + X_CHUNKS[c], W_PASSES):
                 passes = min(W_PASSES, X_CHUNKS[c])
                 loaded.append(
-                    (first_pass, passes, load_weights(nc, w_pool, words_of["q"], 0, len(sums), first_pass, passes))
+                    (first_pass, passes, load_weights(nc, w_pool, words_of["q"], 0, WIDTH, first_pass, passes))
                 )
             if c + 2 < len(X_CHUNKS):
                 load_x(c + 2)
             if c + 1 < len(X_CHUNKS):
                 turn_and_quantise_x(c + 1)
             for first_pass, passes, w in loaded:
-                multiply(nc, w, planes_of["q"], 0, first_pass, passes, x_codes, x_scales, sums)
+                multiply(nc, w, planes_of["q"], 0, N_TILE, first_pass, passes, x_codes, x_scales, sums)
         tables = build_rotation_tables(nc, keep, position_int, {"q": 1.0, "k": HEAD_DIM**-0.5})
-        rotate_block("q", 0, sums, tables)
+        rotate_block("q", 0, N_TILE, sums, tables)
 
-        for half in range(WIDTH // N_TILE):
-            first_column = N_TILE * half
-            sums = open_sums(FIRST_TRANSPOSE_BANK + TOKEN_TILES * half, 1)
-            for first_pass in range(0, PASSES, W_PASSES):
-                w = load_weights(nc, w_pool, words_of["k"], first_column, 1, first_pass, W_PASSES)
-                multiply(nc, w, planes_of["k"], first_column, first_pass, W_PASSES, x_codes, x_scales, sums)
-            rotate_block("k", first_column, sums, tables)
+        first_column = 0
+        for width, passes, first_bank in K_BLOCKS:
+            sums = open_sums(first_bank, 1, width)
+            for first_pass in range(0, PASSES, passes):
+                w = load_weights(nc, w_pool, words_of["k"], first_column, width, first_pass, passes)
+                multiply(nc, w, planes_of["k"], first_column, width, first_pass, passes, x_codes, x_scales, sums)
+            rotate_block("k", first_column, width, sums, tables)
+            first_column += width
 
         for destination, rotated in stores:
             nc.sync.dma_start(out=destination, in_=rotated.rearrange("p h m f -> p h (m f)"))

@@ -99,10 +99,10 @@ def build_rotation_tables(nc, keep, position_int, scale_of):
             in0=trig[:, :, 1, :].unsqueeze(3).to_broadcast([P, TOKEN_TILES, PAIRS, 2]),
             scalar1=scale,
         )
-        sin_cross = keep.tile([P, TOKEN_TILES, 2, PAIRS], F32, name="sin_cross_" + name)
-        nc.vector.tensor_scalar_mul(out=sin_cross[:, :, 0, :], in0=trig[:, :, 0, :], scalar1=-scale)
-        nc.vector.tensor_scalar_mul(out=sin_cross[:, :, 1, :], in0=trig[:, :, 0, :], scalar1=scale)
-        tables[name] = (cos_pairs, sin_cross)
+        sin_pairs = keep.tile([P, TOKEN_TILES, PAIRS, 2], F32, name="sin_pairs_" + name)
+        nc.vector.tensor_scalar_mul(out=sin_pairs[:, :, :, 0], in0=trig[:, :, 0, :], scalar1=-scale)
+        nc.vector.tensor_scalar_mul(out=sin_pairs[:, :, :, 1], in0=trig[:, :, 0, :], scalar1=scale)
+        tables[name] = (cos_pairs, sin_pairs)
     return tables
 
 
@@ -152,6 +152,13 @@ def quantise_x_chunk(nc, grouped, x_codes, x_scales):
     )
 
 
+def weight_loads(first_pass, passes, load_passes, taper):
+    sizes = [min(load_passes, passes)] * (passes // min(load_passes, passes))
+    if taper:
+        sizes = sizes[:-1] + [sizes[-1] - 2] * (sizes[-1] > 2) + [1, 1]
+    return [(first_pass + sum(sizes[:i]), sizes[i]) for i in range(len(sizes))]
+
+
 def load_weights(nc, w_pool, words, first_column, width, first_pass, passes):
     w = w_pool.tile([P, passes, width], U32, tag="w", align_bytes=64)
     nc.sync.dma_start(
@@ -182,32 +189,30 @@ def multiply(nc, w, planes, first_column, tile_width, first_pass, passes, x_code
                 )
 
 
-def rotate_bank(nc, cross_pool, bank, heads, cos_pairs, sin_cross, rotated):
-    by_head = bank.rearrange("p (h f) -> p h f", h=heads)
-    by_pair = bank.rearrange("p (h c e) -> p h c e", h=heads, e=2)
-    nc.vector.tensor_tensor(
-        out=rotated,
-        in0=by_head,
-        in1=cos_pairs.rearrange("p c e -> p (c e)")
-        .unsqueeze(1)
-        .to_broadcast([P, heads, HEAD_DIM]),
-        op=ALU.mult,
-    )
-    cross = cross_pool.tile([P, 2, heads, PAIRS], F32)
-    for e in range(2):
+def rotate_banks(nc, cross_pool, banks, heads, cos_pairs, sin_pairs, rotated):
+    crosses = []
+    for m in range(TOKEN_TILES):
         nc.vector.tensor_tensor(
-            out=cross[:, e],
-            in0=by_pair[:, :, :, 1 - e],
-            in1=sin_cross[:, e, :].unsqueeze(1).to_broadcast([P, heads, PAIRS]),
+            out=rotated[:, :, m, :],
+            in0=banks[m].rearrange("p (h f) -> p h f", h=heads),
+            in1=cos_pairs[:, m].rearrange("p c e -> p (c e)").unsqueeze(1).to_broadcast([P, heads, HEAD_DIM]),
             op=ALU.mult,
         )
-    rotated_pairs = rotated.rearrange("p h (c e) -> p h c e", e=2)
-    nc.vector.tensor_tensor(
-        out=rotated_pairs,
-        in0=rotated_pairs,
-        in1=cross.rearrange("p e h c -> p h c e"),
-        op=ALU.add,
-    )
+        cross = cross_pool.tile([P, heads, PAIRS, 2], F32, tag="cross")
+        nc.vector.tensor_tensor(
+            out=cross,
+            in0=banks[m].rearrange("p (h c e) -> p h c e", h=heads, e=2)[:, :, :, ::-1],
+            in1=sin_pairs[:, m].unsqueeze(1).to_broadcast([P, heads, PAIRS, 2]),
+            op=ALU.mult,
+        )
+        crosses.append(cross)
+    for m in range(TOKEN_TILES):
+        nc.vector.tensor_tensor(
+            out=rotated[:, :, m, :],
+            in0=rotated[:, :, m, :],
+            in1=crosses[m].rearrange("p h c e -> p h (c e)"),
+            op=ALU.add,
+        )
 
 
 def tile_retnet_pa_k_kernel(tc, x, wq_words, wq_scales, wk_words, wk_scales, out_0, out_1):
@@ -274,7 +279,7 @@ def tile_retnet_pa_k_kernel(tc, x, wq_words, wq_scales, wk_words, wk_scales, out
         stores = []
 
         def rotate_block(name, first_column, tile_width, sums, tables):
-            cos_pairs, sin_cross = tables[name]
+            cos_pairs, sin_pairs = tables[name]
             heads = tile_width // HEAD_DIM
             for n in range(len(sums)):
                 rotated = keep.tile(
@@ -282,10 +287,7 @@ def tile_retnet_pa_k_kernel(tc, x, wq_words, wq_scales, wk_words, wk_scales, out
                     F32,
                     name="rotated_%s_%d" % (name, first_column + tile_width * n),
                 )
-                for m in range(TOKEN_TILES):
-                    rotate_bank(
-                        nc, cross_pool, sums[n][m], heads, cos_pairs[:, m], sin_cross[:, m], rotated[:, :, m, :]
-                    )
+                rotate_banks(nc, cross_pool, sums[n], heads, cos_pairs, sin_pairs, rotated)
                 first_head = (first_column + tile_width * n) // HEAD_DIM
                 stores.append((out_of[name][:, first_head : first_head + heads, :], rotated))
 
@@ -317,8 +319,8 @@ def tile_retnet_pa_k_kernel(tc, x, wq_words, wq_scales, wk_words, wk_scales, out
         turn_and_quantise_x(0)
         for c in range(len(X_CHUNKS)):
             loaded = []
-            for first_pass in range(first_pass_of[c], first_pass_of[c] + X_CHUNKS[c], W_PASSES):
-                passes = min(W_PASSES, X_CHUNKS[c])
+            last_of_q = c == len(X_CHUNKS) - 1
+            for first_pass, passes in weight_loads(first_pass_of[c], X_CHUNKS[c], W_PASSES, last_of_q):
                 loaded.append(
                     (first_pass, passes, load_weights(nc, w_pool, words_of["q"], 0, WIDTH, first_pass, passes))
                 )
@@ -332,9 +334,10 @@ def tile_retnet_pa_k_kernel(tc, x, wq_words, wq_scales, wk_words, wk_scales, out
         rotate_block("q", 0, N_TILE, sums, tables)
 
         first_column = 0
-        for width, passes, first_bank in K_BLOCKS:
+        for width, load_passes, first_bank in K_BLOCKS:
             sums = open_sums(first_bank, 1, width)
-            for first_pass in range(0, PASSES, passes):
+            last_of_k = first_column + width == WIDTH
+            for first_pass, passes in weight_loads(0, PASSES, load_passes, last_of_k):
                 w = load_weights(nc, w_pool, words_of["k"], first_column, width, first_pass, passes)
                 multiply(nc, w, planes_of["k"], first_column, width, first_pass, passes, x_codes, x_scales, sums)
             rotate_block("k", first_column, width, sums, tables)

@@ -30,6 +30,7 @@ HEADS_PER_BANK = N_TILE // HEAD_DIM
 X_CHUNKS = (1, 1, 2, 4, 4, 4)
 MAX_X_PASSES = 4
 W_PASSES = 2
+APART_PASSES = 8
 K_BLOCKS = ((512, 2, 4), (256, 4, 6), (256, 2, 0))
 PLANES = 4
 QUADRANT = 32
@@ -168,28 +169,29 @@ def load_weights(nc, w_pool, words, first_column, width, first_pass, passes):
     return w
 
 
-def multiply(nc, w, planes, first_column, tile_width, first_pass, passes, x_codes, x_scales, sums):
+def multiply(nc, loaded, planes, first_column, tile_width, x_codes, x_scales, sums):
     for n in range(len(sums)):
         for m in range(TOKEN_TILES):
-            for i in range(passes):
-                g = first_pass + i
-                plane_start = PACK * (g % PLANES)
-                nc.tensor.matmul_mx(
-                    out=sums[n][m],
-                    lhsT=x_codes[:, g, P * m : P * (m + 1)].bitcast(FP8X4),
-                    lhsT_scale=x_scales[:, g, P * m : P * (m + 1)],
-                    rhs=w[:, i, tile_width * n : tile_width * (n + 1)].bitcast(FP8X4),
-                    rhs_scale=planes[
-                        plane_start:P,
-                        g // PLANES,
-                        first_column + tile_width * n : first_column + tile_width * (n + 1),
-                    ],
-                    start=(g == 0),
-                    stop=(g == PASSES - 1),
-                )
+            for first_pass, passes, w in loaded:
+                for i in range(passes):
+                    g = first_pass + i
+                    plane_start = PACK * (g % PLANES)
+                    nc.tensor.matmul_mx(
+                        out=sums[n][m],
+                        lhsT=x_codes[:, g, P * m : P * (m + 1)].bitcast(FP8X4),
+                        lhsT_scale=x_scales[:, g, P * m : P * (m + 1)],
+                        rhs=w[:, i, tile_width * n : tile_width * (n + 1)].bitcast(FP8X4),
+                        rhs_scale=planes[
+                            plane_start:P,
+                            g // PLANES,
+                            first_column + tile_width * n : first_column + tile_width * (n + 1),
+                        ],
+                        start=(g == 0),
+                        stop=(g == PASSES - 1),
+                    )
 
 
-def rotate_banks(nc, cross_pool, banks, heads, cos_pairs, sin_pairs, rotated):
+def rotate_banks(nc, cross_pool, banks, heads, cos_pairs, sin_pairs, rotated, bank_by_bank):
     crosses = []
     for m in range(TOKEN_TILES):
         nc.vector.tensor_tensor(
@@ -206,13 +208,14 @@ def rotate_banks(nc, cross_pool, banks, heads, cos_pairs, sin_pairs, rotated):
             op=ALU.mult,
         )
         crosses.append(cross)
-    for m in range(TOKEN_TILES):
-        nc.vector.tensor_tensor(
-            out=rotated[:, :, m, :],
-            in0=rotated[:, :, m, :],
-            in1=crosses[m].rearrange("p h c e -> p h (c e)"),
-            op=ALU.add,
-        )
+        if bank_by_bank or m == TOKEN_TILES - 1:
+            for done in range(m if bank_by_bank else 0, m + 1):
+                nc.vector.tensor_tensor(
+                    out=rotated[:, :, done, :],
+                    in0=rotated[:, :, done, :],
+                    in1=crosses[done].rearrange("p h c e -> p h (c e)"),
+                    op=ALU.add,
+                )
 
 
 def tile_retnet_pa_k_kernel(tc, x, wq_words, wq_scales, wk_words, wk_scales, out_0, out_1):
@@ -278,7 +281,7 @@ def tile_retnet_pa_k_kernel(tc, x, wq_words, wq_scales, wk_words, wk_scales, out
 
         stores = []
 
-        def rotate_block(name, first_column, tile_width, sums, tables):
+        def rotate_block(name, first_column, tile_width, sums, tables, bank_by_bank):
             cos_pairs, sin_pairs = tables[name]
             heads = tile_width // HEAD_DIM
             for n in range(len(sums)):
@@ -287,9 +290,15 @@ def tile_retnet_pa_k_kernel(tc, x, wq_words, wq_scales, wk_words, wk_scales, out
                     F32,
                     name="rotated_%s_%d" % (name, first_column + tile_width * n),
                 )
-                rotate_banks(nc, cross_pool, sums[n], heads, cos_pairs, sin_pairs, rotated)
+                rotate_banks(nc, cross_pool, sums[n], heads, cos_pairs, sin_pairs, rotated, bank_by_bank)
                 first_head = (first_column + tile_width * n) // HEAD_DIM
-                stores.append((out_of[name][:, first_head : first_head + heads, :], rotated))
+                destination = out_of[name][:, first_head : first_head + heads, :]
+                if bank_by_bank:
+                    by_token = destination.rearrange("p h (m f) -> p h m f", m=TOKEN_TILES)
+                    for m in range(TOKEN_TILES):
+                        stores.append((by_token[:, :, m, :], rotated[:, :, m, :]))
+                else:
+                    stores.append((destination, rotated.rearrange("p h m f -> p h (m f)")))
 
         first_pass_of = [sum(X_CHUNKS[:c]) for c in range(len(X_CHUNKS))]
         x_chunks = {}
@@ -328,20 +337,26 @@ def tile_retnet_pa_k_kernel(tc, x, wq_words, wq_scales, wk_words, wk_scales, out
                 load_x(c + 2)
             if c + 1 < len(X_CHUNKS):
                 turn_and_quantise_x(c + 1)
-            for first_pass, passes, w in loaded:
-                multiply(nc, w, planes_of["q"], 0, N_TILE, first_pass, passes, x_codes, x_scales, sums)
+            for load in loaded:
+                multiply(nc, [load], planes_of["q"], 0, N_TILE, x_codes, x_scales, sums)
         tables = build_rotation_tables(nc, keep, position_int, {"q": 1.0, "k": HEAD_DIM**-0.5})
-        rotate_block("q", 0, N_TILE, sums, tables)
+        rotate_block("q", 0, N_TILE, sums, tables, False)
 
         first_column = 0
         for width, load_passes, first_bank in K_BLOCKS:
             sums = open_sums(first_bank, 1, width)
             last_of_k = first_column + width == WIDTH
-            for first_pass, passes in weight_loads(0, PASSES, load_passes, last_of_k):
+            held = []
+            for first_pass, passes in weight_loads(0, PASSES, load_passes, False):
                 w = load_weights(nc, w_pool, words_of["k"], first_column, width, first_pass, passes)
-                multiply(nc, w, planes_of["k"], first_column, width, first_pass, passes, x_codes, x_scales, sums)
-            rotate_block("k", first_column, width, sums, tables)
+                if last_of_k and first_pass >= PASSES - APART_PASSES:
+                    held.append((first_pass, passes, w))
+                else:
+                    multiply(nc, [(first_pass, passes, w)], planes_of["k"], first_column, width, x_codes, x_scales, sums)
+            if held:
+                multiply(nc, held, planes_of["k"], first_column, width, x_codes, x_scales, sums)
+            rotate_block("k", first_column, width, sums, tables, last_of_k)
             first_column += width
 
         for destination, rotated in stores:
-            nc.sync.dma_start(out=destination, in_=rotated.rearrange("p h m f -> p h (m f)"))
+            nc.sync.dma_start(out=destination, in_=rotated)

import math
from contextlib import ExitStack

import concourse.mybir as mybir
from concourse.masks import make_identity

F32 = mybir.dt.float32
BF16 = mybir.dt.bfloat16
I32 = mybir.dt.int32
U32 = mybir.dt.uint32
U8 = mybir.dt.uint8
FP8X4 = mybir.dt.float8_e4m3fn_x4
ALU = mybir.AluOpType
ACT = mybir.ActivationFunctionType

P = 128
TOKENS = 256
TOKEN_TILES = TOKENS // P
EMBED = 8192
HEADS = 8
HEAD_DIM = 128
PAIRS = HEAD_DIM // 2
DOUBLINGS = 6
WIDTH = HEADS * HEAD_DIM
PACK = 4
K_PASS = P * PACK
PASSES = EMBED // K_PASS
N_TILE = 512
HEADS_PER_BANK = N_TILE // HEAD_DIM
X_CHUNKS = (1, 1, 2, 4, 4, 4)
MAX_X_PASSES = 4
W_PASSES = 2
APART_PASSES = 8
K_BLOCKS = ((512, 2, 4), (256, 4, 6), (256, 2, 0))
PLANES = 4
QUADRANT = 32
FIRST_TRANSPOSE_BANK = 4

FLOPS = 2 * TOKENS * EMBED * 2 * WIDTH

assert 2**DOUBLINGS == PAIRS
assert sum(X_CHUNKS) == PASSES and max(X_CHUNKS) <= MAX_X_PASSES


def build_rotation_tables(nc, keep, position_int, scale_of):
    position = keep.tile([P, TOKEN_TILES], F32)
    nc.vector.tensor_copy(out=position, in_=position_int)

    ratio = 10000.0 ** (-1.0 / (PAIRS - 1))
    angle = keep.tile([P, PAIRS], F32)
    nc.vector.memset(angle[:, 0:1], 1.0)
    for doubling in range(DOUBLINGS):
        done = 2**doubling
        nc.vector.tensor_scalar_mul(
            out=angle[:, done : 2 * done], in0=angle[:, 0:done], scalar1=ratio**done
        )

    phase = keep.tile([P, TOKEN_TILES, 2, PAIRS], F32)
    for m in range(TOKEN_TILES):
        for kind, shift in enumerate((0.0, math.pi / 2)):
            nc.vector.tensor_scalar(
                out=phase[:, m, kind, :],
                in0=angle,
                scalar1=position[:, m : m + 1],
                scalar2=shift,
                op0=ALU.mult,
                op1=ALU.add,
            )

    half_turns_int = keep.tile([P, TOKEN_TILES, 2, PAIRS], I32)
    nc.vector.tensor_scalar_mul(out=half_turns_int, in0=phase, scalar1=1.0 / math.pi)
    half_turns = keep.tile([P, TOKEN_TILES, 2, PAIRS], F32)
    nc.vector.tensor_copy(out=half_turns, in_=half_turns_int)
    pi_high = 3.140625
    pi_low = math.pi - pi_high
    reduced = keep.tile([P, TOKEN_TILES, 2, PAIRS], F32)
    nc.vector.scalar_tensor_tensor(
        out=reduced, in0=half_turns, scalar=-pi_high, in1=phase, op0=ALU.mult, op1=ALU.add
    )
    nc.vector.scalar_tensor_tensor(
        out=reduced, in0=half_turns, scalar=-pi_low, in1=reduced, op0=ALU.mult, op1=ALU.add
    )
    sine = keep.tile([P, TOKEN_TILES, 2, PAIRS], F32)
    nc.scalar.activation(out=sine, in_=reduced, func=ACT.Sin)

    odd_int = keep.tile([P, TOKEN_TILES, 2, PAIRS], I32)
    nc.vector.tensor_single_scalar(out=odd_int, in_=half_turns_int, scalar=1, op=ALU.bitwise_and)
    sign = keep.tile([P, TOKEN_TILES, 2, PAIRS], F32)
    nc.vector.tensor_scalar(
        out=sign, in0=odd_int, scalar1=-2.0, scalar2=1.0, op0=ALU.mult, op1=ALU.add
    )
    trig = keep.tile([P, TOKEN_TILES, 2, PAIRS], F32)
    nc.vector.tensor_tensor(out=trig, in0=sine, in1=sign, op=ALU.mult)

    tables = {}
    for name, scale in scale_of.items():
        cos_pairs = keep.tile([P, TOKEN_TILES, PAIRS, 2], F32, name="cos_pairs_" + name)
        nc.vector.tensor_scalar_mul(
            out=cos_pairs,
            in0=trig[:, :, 1, :].unsqueeze(3).to_broadcast([P, TOKEN_TILES, PAIRS, 2]),
            scalar1=scale,
        )
        sin_pairs = keep.tile([P, TOKEN_TILES, PAIRS, 2], F32, name="sin_pairs_" + name)
        nc.vector.tensor_scalar_mul(out=sin_pairs[:, :, :, 0], in0=trig[:, :, 0, :], scalar1=-scale)
        nc.vector.tensor_scalar_mul(out=sin_pairs[:, :, :, 1], in0=trig[:, :, 0, :], scalar1=scale)
        tables[name] = (cos_pairs, sin_pairs)
    return tables


def load_scale_planes(queue, planes, scales, group):
    for quadrant in range(P // QUADRANT):
        first = QUADRANT * quadrant
        queue.dma_start(
            out=planes[first : first + PACK * PLANES, group, :].bitcast(F32),
            in_=scales[
                PLANES * group : PLANES * (group + 1), PACK * quadrant : PACK * (quadrant + 1), :
            ].bitcast(F32),
        )


def turn_x_chunk(nc, sorted_pool, grouped_pool, psum, identity, x_chunk, first_pass, passes):
    words = x_chunk.bitcast(F32)
    if passes > 1:
        sorted_words = sorted_pool.tile([P, TOKEN_TILES, passes, 2, P], F32, tag="sorted_words")
        for m in range(TOKEN_TILES):
            sort = nc.vector.tensor_copy if m % 2 == 0 else nc.scalar.copy
            sort(out=sorted_words[:, m], in_=words[:, m].rearrange("p (j w u) -> p j u w", w=P, u=2))
    grouped = grouped_pool.tile([P, passes, TOKENS, PACK], BF16, tag="grouped", align_bytes=64)
    grouped_words = grouped.bitcast(F32)
    for j in range(passes):
        bank = FIRST_TRANSPOSE_BANK + (first_pass + j) % MAX_X_PASSES
        turned = psum.tile([P, TOKEN_TILES, 2, P], F32, tag="bank%d" % bank, name="turned")
        for m in range(TOKEN_TILES):
            for u in range(2):
                if passes > 1:
                    source = sorted_words[:, m, j, u, :]
                else:
                    source = words[:, m, u : 2 * P : 2]
                nc.tensor.transpose(turned[:, m, u, :], source, identity)
        copy_out = nc.vector.tensor_copy if (j % 2 == 0 and passes > 1) else nc.scalar.copy
        copy_out(
            out=grouped_words[:, j].rearrange("p (m r) u -> p m r u", m=TOKEN_TILES),
            in_=turned.rearrange("p m u r -> p m r u"),
        )
    return grouped


def quantise_x_chunk(nc, grouped, x_codes, x_scales):
    nc.vector.quantize_mx(
        out=x_codes.rearrange("p g r -> p (g r)").bitcast(FP8X4),
        scales=x_scales.rearrange("p g r -> p (g r)"),
        in_=grouped.rearrange("p g r t -> p (g r t)"),
    )


def weight_loads(first_pass, passes, load_passes, taper):
    sizes = [min(load_passes, passes)] * (passes // min(load_passes, passes))
    if taper:
        sizes = sizes[:-1] + [sizes[-1] - 2] * (sizes[-1] > 2) + [1, 1]
    return [(first_pass + sum(sizes[:i]), sizes[i]) for i in range(len(sizes))]


def load_weights(nc, w_pool, words, first_column, width, first_pass, passes):
    w = w_pool.tile([P, passes, width], U32, tag="w", align_bytes=64)
    nc.sync.dma_start(
        out=w.bitcast(I32),
        in_=words[:, first_pass : first_pass + passes, first_column : first_column + width],
    )
    return w


def multiply(nc, loaded, planes, first_column, tile_width, x_codes, x_scales, sums):
    for n in range(len(sums)):
        for m in range(TOKEN_TILES):
            for first_pass, passes, w in loaded:
                for i in range(passes):
                    g = first_pass + i
                    plane_start = PACK * (g % PLANES)
                    nc.tensor.matmul_mx(
                        out=sums[n][m],
                        lhsT=x_codes[:, g, P * m : P * (m + 1)].bitcast(FP8X4),
                        lhsT_scale=x_scales[:, g, P * m : P * (m + 1)],
                        rhs=w[:, i, tile_width * n : tile_width * (n + 1)].bitcast(FP8X4),
                        rhs_scale=planes[
                            plane_start:P,
                            g // PLANES,
                            first_column + tile_width * n : first_column + tile_width * (n + 1),
                        ],
                        start=(g == 0),
                        stop=(g == PASSES - 1),
                    )


def rotate_banks(nc, cross_pool, banks, heads, cos_pairs, sin_pairs, rotated, bank_by_bank):
    crosses = []
    for m in range(TOKEN_TILES):
        nc.vector.tensor_tensor(
            out=rotated[:, :, m, :],
            in0=banks[m].rearrange("p (h f) -> p h f", h=heads),
            in1=cos_pairs[:, m].rearrange("p c e -> p (c e)").unsqueeze(1).to_broadcast([P, heads, HEAD_DIM]),
            op=ALU.mult,
        )
        cross = cross_pool.tile([P, heads, PAIRS, 2], F32, tag="cross")
        nc.vector.tensor_tensor(
            out=cross,
            in0=banks[m].rearrange("p (h c e) -> p h c e", h=heads, e=2)[:, :, :, ::-1],
            in1=sin_pairs[:, m].unsqueeze(1).to_broadcast([P, heads, PAIRS, 2]),
            op=ALU.mult,
        )
        crosses.append(cross)
        if bank_by_bank or m == TOKEN_TILES - 1:
            for done in range(m if bank_by_bank else 0, m + 1):
                nc.vector.tensor_tensor(
                    out=rotated[:, :, done, :],
                    in0=rotated[:, :, done, :],
                    in1=crosses[done].rearrange("p h c e -> p h (c e)"),
                    op=ALU.add,
                )


def tile_retnet_pa_k_kernel(tc, x, wq_words, wq_scales, wk_words, wk_scales, out_0, out_1):
    nc = tc.nc
    with ExitStack() as ctx:
        ctx.enter_context(tc.manual_schedule())
        keep = ctx.enter_context(tc.tile_pool(name="keep", bufs=1))
        sorted_pool = ctx.enter_context(tc.tile_pool(name="sorted", bufs=2))
        grouped_pool = ctx.enter_context(tc.tile_pool(name="grouped", bufs=2))
        w_pool = ctx.enter_context(tc.tile_pool(name="w", bufs=12))
        cross_pool = ctx.enter_context(tc.tile_pool(name="cross", bufs=2))
        psum = ctx.enter_context(tc.psum_pool(name="psum", bufs=1))

        x_rows = x.rearrange("b (p m) k -> p (b m) k", m=TOKEN_TILES)
        words_of = {
            "q": wq_words.rearrange("g p n t -> p g (n t)").bitcast(I32),
            "k": wk_words.rearrange("g p n t -> p g (n t)").bitcast(I32),
        }
        scales_of = {"q": wq_scales, "k": wk_scales}
        out_of = {
            "q": out_0.rearrange("b h (p m) f -> p (b h) (m f)", m=TOKEN_TILES),
            "k": out_1.rearrange("b h (p m) f -> p (b h) (m f)", m=TOKEN_TILES),
        }

        planes_of = {}
        for name in ("q", "k"):
            planes_of[name] = keep.tile(
                [P, PASSES // PLANES, WIDTH], U8, name="planes_" + name, align_bytes=64
            )
        zero = keep.tile([P, 1], F32)
        nc.vector.memset(planes_of["q"][:, 0, :].bitcast(I32), 0)
        nc.vector.memset(zero, 0.0)
        nc.vector.memset(planes_of["q"][:, 1:, :].bitcast(I32), 0)
        nc.vector.memset(planes_of["k"].bitcast(I32), 0)
        load_scale_planes(nc.scalar, planes_of["q"], scales_of["q"], 0)

        identity = keep.tile([P, P], F32)
        make_identity(nc, identity)
        position_int = keep.tile([P, TOKEN_TILES], I32)
        nc.gpsimd.iota(
            position_int, pattern=[[1, TOKEN_TILES]], base=0, channel_multiplier=TOKEN_TILES
        )
        for name in ("q", "k"):
            for group in range(PASSES // PLANES):
                if (name, group) != ("q", 0):
                    load_scale_planes(nc.gpsimd, planes_of[name], scales_of[name], group)

        x_codes = keep.tile([P, PASSES, TOKENS], U32, align_bytes=64)
        x_scales = keep.tile([P, PASSES, TOKENS], U8, align_bytes=64)

        def open_sums(first_bank, n_tiles, tile_width):
            return [
                [
                    psum.tile(
                        [P, tile_width], F32, tag="bank%d" % (first_bank + TOKEN_TILES * n + m), name="sums"
                    )
                    for m in range(TOKEN_TILES)
                ]
                for n in range(n_tiles)
            ]

        nc.scalar.activation(out=zero, in_=zero, func=ACT.Sin)

        stores = []

        def rotate_block(name, first_column, tile_width, sums, tables, bank_by_bank):
            cos_pairs, sin_pairs = tables[name]
            heads = tile_width // HEAD_DIM
            for n in range(len(sums)):
                rotated = keep.tile(
                    [P, heads, TOKEN_TILES, HEAD_DIM],
                    F32,
                    name="rotated_%s_%d" % (name, first_column + tile_width * n),
                )
                rotate_banks(nc, cross_pool, sums[n], heads, cos_pairs, sin_pairs, rotated, bank_by_bank)
                first_head = (first_column + tile_width * n) // HEAD_DIM
                destination = out_of[name][:, first_head : first_head + heads, :]
                if bank_by_bank:
                    by_token = destination.rearrange("p h (m f) -> p h m f", m=TOKEN_TILES)
                    for m in range(TOKEN_TILES):
                        stores.append((by_token[:, :, m, :], rotated[:, :, m, :]))
                else:
                    stores.append((destination, rotated.rearrange("p h m f -> p h (m f)")))

        first_pass_of = [sum(X_CHUNKS[:c]) for c in range(len(X_CHUNKS))]
        x_chunks = {}

        def load_x(c):
            first_k = K_PASS * first_pass_of[c]
            x_chunks[c] = keep.tile([P, TOKEN_TILES, X_CHUNKS[c] * K_PASS], BF16, name="x_chunk_%d" % c)
            nc.sync.dma_start(
                out=x_chunks[c], in_=x_rows[:, :, first_k : first_k + X_CHUNKS[c] * K_PASS]
            )

        def turn_and_quantise_x(c):
            first_pass = first_pass_of[c]
            grouped = turn_x_chunk(
                nc, sorted_pool, grouped_pool, psum, identity, x_chunks[c], first_pass, X_CHUNKS[c]
            )
            quantise_x_chunk(
                nc,
                grouped,
                x_codes[:, first_pass : first_pass + X_CHUNKS[c], :],
                x_scales[:, first_pass : first_pass + X_CHUNKS[c], :],
            )

        sums = open_sums(0, WIDTH // N_TILE, N_TILE)
        load_x(0)
        load_x(1)
        turn_and_quantise_x(0)
        for c in range(len(X_CHUNKS)):
            loaded = []
            last_of_q = c == len(X_CHUNKS) - 1
            for first_pass, passes in weight_loads(first_pass_of[c], X_CHUNKS[c], W_PASSES, last_of_q):
                loaded.append(
                    (first_pass, passes, load_weights(nc, w_pool, words_of["q"], 0, WIDTH, first_pass, passes))
                )
            if c + 2 < len(X_CHUNKS):
                load_x(c + 2)
            if c + 1 < len(X_CHUNKS):
                turn_and_quantise_x(c + 1)
            for load in loaded:
                multiply(nc, [load], planes_of["q"], 0, N_TILE, x_codes, x_scales, sums)
        tables = build_rotation_tables(nc, keep, position_int, {"q": 1.0, "k": HEAD_DIM**-0.5})
        rotate_block("q", 0, N_TILE, sums, tables, False)

        first_column = 0
        for width, load_passes, first_bank in K_BLOCKS:
            sums = open_sums(first_bank, 1, width)
            last_of_k = first_column + width == WIDTH
            held = []
            for first_pass, passes in weight_loads(0, PASSES, load_passes, False):
                w = load_weights(nc, w_pool, words_of["k"], first_column, width, first_pass, passes)
                if last_of_k and first_pass >= PASSES - APART_PASSES:
                    held.append((first_pass, passes, w))
                else:
                    multiply(nc, [(first_pass, passes, w)], planes_of["k"], first_column, width, x_codes, x_scales, sums)
            if held:
                multiply(nc, held, planes_of["k"], first_column, width, x_codes, x_scales, sums)
            rotate_block("k", first_column, width, sums, tables, last_of_k)
            first_column += width

        for destination, rotated in stores:
            nc.sync.dma_start(out=destination, in_=rotated)
